import numpy as np
import ml_dtypes


def mxq(x, axis, fmt="e4m3"):
    dtype, down = {"e4m3": (ml_dtypes.float8_e4m3fn, 7), "e5m2": (ml_dtypes.float8_e5m2, 14)}[fmt]
    v = np.moveaxis(np.asarray(x, np.float32).astype(ml_dtypes.bfloat16).astype(np.float64), axis, -1)
    blocks = v.reshape(v.shape[:-1] + (-1, 32))
    amax = np.abs(blocks).max(-1, keepdims=True)
    byte = np.maximum(np.where(amax > 0, np.frexp(amax)[1] - 1 + 127, 0) - down, 1)
    scale = np.exp2(byte - 127.0)
    codes = (blocks / scale).astype(np.float32).astype(dtype).astype(np.float64)
    return np.moveaxis((codes * scale).reshape(v.shape), -1, axis)


WIDE = False


def mx_kscale(k):
    if not WIDE:
        return np.ones(k)
    levels = np.array([10, -10, 5, -5, 0])
    a = np.random.permutation(np.resize(levels, k // 512 * 4)).reshape(k // 512, 4)
    idx = np.arange(k)
    return np.exp2(a[idx // 512, idx % 128 // 32])


BF16 = ml_dtypes.bfloat16


def bf(x):
    return np.asarray(x, np.float32).astype(BF16)


def f64(x):
    return np.asarray(x).astype(np.float64)


B, N, H, F, M, G, C = 8, 16, 512, 8192, 256, 1024, 3


def silu(v):
    return v / (1.0 + np.exp(-v))


def setup_inputs():
    s = mx_kscale(H)
    w_nodes = np.random.standard_normal((2, H, F)) / np.sqrt(2 * H) / s[None, :, None]
    w_dist = np.random.standard_normal((1, F)) * 0.3
    return {"node_state": bf(np.random.standard_normal((B, N, H)) * s),
            "positions": bf(np.random.standard_normal((B, N, C))),
            "We1": bf(np.concatenate([w_nodes.reshape(2 * H, F), w_dist], 0)),
            "be1": bf(np.random.standard_normal(F) * 0.5),
            "We2": bf(np.random.standard_normal((F, M)) / np.sqrt(F)),
            "be2": bf(np.random.standard_normal(M) * 0.5)}


def reference(node_state, positions, We1, be1, We2, be2):
    x, p, w1 = f64(node_state), f64(positions), f64(We1)
    rel = p[:, :, None, :] - p[:, None, :, :]
    sq = np.sum(rel * rel, axis=-1, keepdims=True)
    dist = np.where(sq > 0, np.sqrt(np.where(sq > 0, sq, 1.0)), 0.0)
    xq = mxq(x, 2, "e4m3")
    a_i = xq @ mxq(w1[:H], 0, "e4m3")
    a_j = xq @ mxq(w1[H:2 * H], 0, "e4m3")
    pre = a_i[:, :, None, :] + a_j[:, None, :, :] + dist * w1[2 * H] + f64(be1)
    h = silu(pre).reshape(B * N * N, F)
    msg = (mxq(h, 1, "e4m3") @ mxq(f64(We2), 0, "e4m3")) + f64(be2)
    return msg.reshape(B, N, N, M)

@@ -1,0 +1,255 @@
+from contextlib import ExitStack
+
+import concourse.mybir as mybir
+from concourse.masks import make_identity
+
+F32 = mybir.dt.float32
+BF16 = mybir.dt.bfloat16
+U32 = mybir.dt.uint32
+U8 = mybir.dt.uint8
+FP8X4 = mybir.dt.float8_e4m3fn_x4
+ALU = mybir.AluOpType
+ACT = mybir.ActivationFunctionType
+
+P = 128
+PACK = 4
+K_PASS = P * PACK
+
+GRAPHS = 8
+NODES_PER_GRAPH = 16
+NODES = GRAPHS * NODES_PER_GRAPH
+COORDS = 3
+FEATURES = 512
+HIDDEN = 8192
+MESSAGE = 256
+
+HIDDEN_PASSES = HIDDEN // K_PASS
+HIDDEN_TILES = HIDDEN // P
+J_PER_CHUNK = 4
+EDGE_CHUNK = J_PER_CHUNK * NODES
+EDGE_CHUNKS = NODES_PER_GRAPH // J_PER_CHUNK
+WE1_COLS = 1024
+WE2_PASSES = 4
+RUN = 4
+
+SMALLEST_SQUARE = 2.0 ** -100
+
+FLOPS = 2 * NODES * 2 * FEATURES * HIDDEN + 2 * NODES * NODES_PER_GRAPH * HIDDEN * MESSAGE
+
+
+def regroup(copy, grouped, rows):
+    copy(
+        out=grouped.rearrange("p (c i) t -> p c t i", i=RUN),
+        in_=rows.rearrange("p t (c i) -> p c t i", i=RUN),
+    )
+
+
+def tile_graphmessagelayer_pa_k_kernel(tc, node_state, positions, We1, be1, We2, be2, out):
+    nc = tc.nc
+    with ExitStack() as ctx:
+        keep = ctx.enter_context(tc.tile_pool(name="keep", bufs=1))
+        loads = ctx.enter_context(tc.tile_pool(name="loads", bufs=3))
+        groupeds = ctx.enter_context(tc.tile_pool(name="groupeds", bufs=2))
+        work = ctx.enter_context(tc.tile_pool(name="work", bufs=2))
+        banks = ctx.enter_context(tc.psum_pool(name="banks", bufs=4))
+        sums = ctx.enter_context(tc.psum_pool(name="sums", bufs=1))
+
+        x_rows = keep.tile([P, FEATURES], BF16)
+        nc.sync.dma_start(out=x_rows[:], in_=node_state.rearrange("b n h -> (b n) h"))
+        pos_own = keep.tile([P, COORDS], BF16)
+        nc.scalar.dma_start(out=pos_own[:], in_=positions.rearrange("b n c -> (b n) c"))
+        pos_graph = keep.tile([P, NODES_PER_GRAPH * COORDS], BF16)
+        for b in range(GRAPHS):
+            nc.scalar.dma_start(
+                out=pos_graph[b * NODES_PER_GRAPH : (b + 1) * NODES_PER_GRAPH, :],
+                in_=positions[b].rearrange("n c -> (n c)").partition_broadcast(NODES_PER_GRAPH),
+            )
+        vec_rows = keep.tile([P, P], BF16)
+        nc.scalar.dma_start(
+            out=vec_rows[0:HIDDEN_TILES, :],
+            in_=We1[2 * FEATURES : 2 * FEATURES + 1, :].rearrange("o (q p) -> (o q) p", p=P),
+        )
+        nc.scalar.dma_start(out=vec_rows[HIDDEN_TILES:P, :], in_=be1.rearrange("(q p) -> q p", p=P))
+        be2_all = keep.tile([P, MESSAGE], BF16)
+        nc.scalar.dma_start(out=be2_all[:], in_=be2.partition_broadcast(P))
+
+        ident_bf16 = keep.tile([P, P], BF16)
+        make_identity(nc, ident_bf16[:])
+        ident_f32 = keep.tile([P, P], F32)
+        make_identity(nc, ident_f32[:])
+
+        xT = banks.tile([P, PACK, NODES], BF16, tag="bank")
+        for t in range(PACK):
+            nc.tensor.transpose(out=xT[:, t, :], in_=x_rows[:, t * P : (t + 1) * P], identity=ident_bf16[:])
+        x_words = keep.tile([P, NODES, PACK], BF16)
+        nc.vector.tensor_copy(out=x_words[:], in_=xT[:].rearrange("p t n -> p n t"))
+
+        xi_in = work.tile([P, J_PER_CHUNK, NODES, PACK], BF16, tag="h_bf16", align_bytes=64)
+        nc.vector.tensor_copy(
+            out=xi_in[:], in_=x_words[:].unsqueeze(1).to_broadcast([P, J_PER_CHUNK, NODES, PACK])
+        )
+        xi_codes = keep.tile([P, EDGE_CHUNK], U32, align_bytes=64)
+        xi_scales = keep.tile([P, EDGE_CHUNK], U8, align_bytes=64)
+        nc.vector.quantize_mx(
+            out=xi_codes[:].bitcast(FP8X4),
+            scales=xi_scales[:],
+            in_=xi_in[:].rearrange("p s n t -> p (s n t)"),
+        )
+
+        xj_codes = keep.tile([P, EDGE_CHUNKS, EDGE_CHUNK], U32, align_bytes=64)
+        xj_scales = keep.tile([P, EDGE_CHUNKS, EDGE_CHUNK], U8, align_bytes=64)
+        x_by_graph = x_words[:].rearrange("p (b n) t -> p b n t", n=NODES_PER_GRAPH)
+        for c in range(EDGE_CHUNKS):
+            xj_in = work.tile([P, J_PER_CHUNK, GRAPHS, NODES_PER_GRAPH, PACK], BF16, tag="h_bf16", align_bytes=64)
+            for s in range(J_PER_CHUNK):
+                j = c * J_PER_CHUNK + s
+                nc.vector.tensor_copy(
+                    out=xj_in[:, s],
+                    in_=x_by_graph[:, :, j : j + 1, :].to_broadcast([P, GRAPHS, NODES_PER_GRAPH, PACK]),
+                )
+            nc.vector.quantize_mx(
+                out=xj_codes[:, c, :].bitcast(FP8X4),
+                scales=xj_scales[:, c, :],
+                in_=xj_in[:].rearrange("p s b i t -> p (s b i t)"),
+            )
+
+        vecT = banks.tile([P, P], BF16, tag="bank")
+        nc.tensor.transpose(out=vecT[:], in_=vec_rows[:], identity=ident_bf16[:])
+        vec_cols = keep.tile([P, P], F32)
+        nc.vector.tensor_copy(out=vec_cols[:], in_=vecT[:])
+
+        rel = keep.tile([P, NODES_PER_GRAPH, COORDS], F32)
+        nc.vector.tensor_tensor(
+            out=rel[:],
+            in0=pos_graph[:].rearrange("p (n c) -> p n c", c=COORDS),
+            in1=pos_own[:].unsqueeze(1).to_broadcast([P, NODES_PER_GRAPH, COORDS]),
+            op=ALU.subtract,
+        )
+        rel_sq = keep.tile([P, NODES_PER_GRAPH, COORDS], F32)
+        nc.vector.tensor_tensor(out=rel_sq[:], in0=rel[:], in1=rel[:], op=ALU.mult)
+        sq = keep.tile([P, NODES_PER_GRAPH], F32)
+        nc.vector.tensor_reduce(out=sq[:], in_=rel_sq[:], axis=mybir.AxisListType.X, op=ALU.add)
+        sq_safe = keep.tile([P, NODES_PER_GRAPH], F32)
+        nc.vector.tensor_scalar_max(out=sq_safe[:], in0=sq[:], scalar1=SMALLEST_SQUARE)
+        root = keep.tile([P, NODES_PER_GRAPH], F32)
+        nc.scalar.activation(out=root[:], in_=sq_safe[:], func=ACT.Sqrt)
+        dist = keep.tile([P, NODES_PER_GRAPH], F32)
+        nc.vector.scalar_tensor_tensor(
+            out=dist[:], in0=sq[:], scalar=0.0, in1=root[:], op0=ALU.is_gt, op1=ALU.mult
+        )
+        dist_rep = loads.tile([P, NODES_PER_GRAPH, P], F32, tag="rows")
+        nc.vector.tensor_copy(out=dist_rep[:], in_=dist[:].unsqueeze(2).to_broadcast([P, NODES_PER_GRAPH, P]))
+        dist_all = keep.tile([P, EDGE_CHUNKS, EDGE_CHUNK], F32)
+        for c in range(EDGE_CHUNKS):
+            distT = banks.tile([P, J_PER_CHUNK, NODES], F32, tag="bank")
+            for s in range(J_PER_CHUNK):
+                nc.tensor.transpose(
+                    out=distT[:, s, :], in_=dist_rep[:, c * J_PER_CHUNK + s, :], identity=ident_f32[:]
+                )
+            nc.scalar.copy(out=dist_all[:, c, :], in_=distT[:].rearrange("p s n -> p (s n)"))
+
+        we1_codes = [keep.tile([P, HIDDEN], U32, name="we1_codes%d" % blk, align_bytes=64) for blk in range(2)]
+        we1_scales = [keep.tile([P, HIDDEN], U8, name="we1_scales%d" % blk, align_bytes=64) for blk in range(2)]
+        we2_codes = keep.tile([P, HIDDEN_PASSES, MESSAGE], U32, align_bytes=64)
+        we2_scales = keep.tile([P, HIDDEN_PASSES, MESSAGE], U8, align_bytes=64)
+        we2_view = We2.rearrange("(g t p) m -> p g t m", t=PACK, p=P)
+
+        def quantise_we1(first_col):
+            cols = slice(first_col, first_col + WE1_COLS)
+            for blk, copy in ((0, nc.vector.tensor_copy), (1, nc.scalar.copy)):
+                rows = loads.tile([P, PACK, WE1_COLS], BF16, tag="rows")
+                block = We1[blk * FEATURES : (blk + 1) * FEATURES, :].rearrange("(t p) f -> p t f", p=P)
+                nc.sync.dma_start(out=rows[:], in_=block[:, :, cols])
+                grouped = groupeds.tile([P, WE1_COLS, PACK], BF16, tag="grouped", align_bytes=64)
+                regroup(copy, grouped[:], rows[:])
+                nc.vector.quantize_mx(
+                    out=we1_codes[blk][:, cols].bitcast(FP8X4),
+                    scales=we1_scales[blk][:, cols],
+                    in_=grouped[:].rearrange("p f t -> p (f t)"),
+                )
+
+        def quantise_we2(first_pass):
+            passes = slice(first_pass, first_pass + WE2_PASSES)
+            rows = loads.tile([P, WE2_PASSES, PACK, MESSAGE], BF16, tag="rows")
+            nc.sync.dma_start(out=rows[:], in_=we2_view[:, passes])
+            grouped = groupeds.tile([P, WE2_PASSES, MESSAGE, PACK], BF16, tag="grouped", align_bytes=64)
+            for g in range(WE2_PASSES):
+                regroup(nc.scalar.copy, grouped[:, g], rows[:, g])
+            nc.vector.quantize_mx(
+                out=we2_codes[:, passes, :].rearrange("p g m -> p (g m)").bitcast(FP8X4),
+                scales=we2_scales[:, passes, :].rearrange("p g m -> p (g m)"),
+                in_=grouped[:].rearrange("p g m t -> p (g m t)"),
+            )
+
+        out_rows = out.rearrange("b i j m -> (b i) j m")
+        for c in range(EDGE_CHUNKS):
+            msg = [sums.tile([P, MESSAGE], F32, name="msg%d" % s) for s in range(J_PER_CHUNK)]
+            for g in range(HIDDEN_PASSES):
+                if c == 0 and (g * K_PASS) % WE1_COLS == 0:
+                    quantise_we1(g * K_PASS)
+                if c == 0 and g % WE2_PASSES == 0:
+                    quantise_we2(g)
+
+                dist_term = work.tile([P, PACK, EDGE_CHUNK], F32)
+                pre = work.tile([P, PACK, EDGE_CHUNK], F32)
+                for t in range(PACK):
+                    q = g * PACK + t
+                    f_cols = slice(q * P, (q + 1) * P)
+                    nc.gpsimd.tensor_scalar(
+                        out=dist_term[:, t, :],
+                        in0=dist_all[:, c, :],
+                        scalar1=vec_cols[:, q : q + 1],
+                        scalar2=vec_cols[:, HIDDEN_TILES + q : HIDDEN_TILES + q + 1],
+                        op0=ALU.mult,
+                        op1=ALU.add,
+                    )
+                    node_terms = banks.tile([P, EDGE_CHUNK], F32, tag="bank")
+                    nc.tensor.matmul_mx(
+                        out=node_terms[:],
+                        lhsT=we1_codes[0][:, f_cols].bitcast(FP8X4),
+                        lhsT_scale=we1_scales[0][:, f_cols],
+                        rhs=xi_codes[:].bitcast(FP8X4),
+                        rhs_scale=xi_scales[:],
+                        start=True,
+                        stop=False,
+                    )
+                    nc.tensor.matmul_mx(
+                        out=node_terms[:],
+                        lhsT=we1_codes[1][:, f_cols].bitcast(FP8X4),
+                        lhsT_scale=we1_scales[1][:, f_cols],
+                        rhs=xj_codes[:, c, :].bitcast(FP8X4),
+                        rhs_scale=xj_scales[:, c, :],
+                        start=False,
+                        stop=True,
+                    )
+                    nc.vector.tensor_tensor(out=pre[:, t, :], in0=node_terms[:], in1=dist_term[:, t, :], op=ALU.add)
+
+                h_bf16 = work.tile([P, EDGE_CHUNK, PACK], BF16, align_bytes=64)
+                nc.scalar.activation(
+                    out=h_bf16[:].rearrange("p (c i) t -> p c t i", i=RUN),
+                    in_=pre[:].rearrange("p t (c i) -> p c t i", i=RUN),
+                    func=ACT.Silu,
+                )
+                h_codes = work.tile([P, EDGE_CHUNK], U32, align_bytes=64)
+                h_scales = work.tile([P, EDGE_CHUNK], U8, align_bytes=64)
+                nc.vector.quantize_mx(
+                    out=h_codes[:].bitcast(FP8X4),
+                    scales=h_scales[:],
+                    in_=h_bf16[:].rearrange("p e t -> p (e t)"),
+                )
+                for s in range(J_PER_CHUNK):
+                    e_cols = slice(s * NODES, (s + 1) * NODES)
+                    nc.tensor.matmul_mx(
+                        out=msg[s][:],
+                        lhsT=h_codes[:, e_cols].bitcast(FP8X4),
+                        lhsT_scale=h_scales[:, e_cols],
+                        rhs=we2_codes[:, g, :].bitcast(FP8X4),
+                        rhs_scale=we2_scales[:, g, :],
+                        start=(g == 0),
+                        stop=(g == HIDDEN_PASSES - 1),
+                    )
+
+            result = work.tile([P, J_PER_CHUNK, MESSAGE], F32)
+            for s in range(J_PER_CHUNK):
+                nc.vector.tensor_tensor(out=result[:, s, :], in0=msg[s][:], in1=be2_all[:], op=ALU.add)
+            nc.sync.dma_start(out=out_rows[:, c * J_PER_CHUNK : (c + 1) * J_PER_CHUNK, :], in_=result[:])

@@ -31,6 +31,7 @@ EDGE_CHUNKS = NODES_PER_GRAPH // J_PER_CHUNK
 WE1_COLS = 1024
 WE2_PASSES = 4
 RUN = 4
+SCALAR_PLANE = PACK - 1
 
 SMALLEST_SQUARE = 2.0 ** -100
 
@@ -51,6 +52,8 @@ def tile_graphmessagelayer_pa_k_kernel(tc, node_state, positions, We1, be1, We2,
         loads = ctx.enter_context(tc.tile_pool(name="loads", bufs=3))
         groupeds = ctx.enter_context(tc.tile_pool(name="groupeds", bufs=2))
         work = ctx.enter_context(tc.tile_pool(name="work", bufs=2))
+        terms = ctx.enter_context(tc.tile_pool(name="terms", bufs=6))
+        pres = ctx.enter_context(tc.tile_pool(name="pres", bufs=3))
         banks = ctx.enter_context(tc.psum_pool(name="banks", bufs=4))
         sums = ctx.enter_context(tc.psum_pool(name="sums", bufs=1))
 
@@ -190,19 +193,22 @@ def tile_graphmessagelayer_pa_k_kernel(tc, node_state, positions, We1, be1, We2,
                 if c == 0 and g % WE2_PASSES == 0:
                     quantise_we2(g)
 
-                dist_term = work.tile([P, PACK, EDGE_CHUNK], F32)
-                pre = work.tile([P, PACK, EDGE_CHUNK], F32)
+                pre = pres.tile([P, PACK, EDGE_CHUNK], F32)
                 for t in range(PACK):
                     q = g * PACK + t
                     f_cols = slice(q * P, (q + 1) * P)
-                    nc.gpsimd.tensor_scalar(
-                        out=dist_term[:, t, :],
-                        in0=dist_all[:, c, :],
-                        scalar1=vec_cols[:, q : q + 1],
-                        scalar2=vec_cols[:, HIDDEN_TILES + q : HIDDEN_TILES + q + 1],
-                        op0=ALU.mult,
-                        op1=ALU.add,
-                    )
+                    dist_term = terms.tile([P, EDGE_CHUNK], F32)
+                    w_dist = vec_cols[:, q : q + 1]
+                    bias = vec_cols[:, HIDDEN_TILES + q : HIDDEN_TILES + q + 1]
+                    if t == SCALAR_PLANE:
+                        nc.scalar.activation(
+                            out=dist_term[:], in_=dist_all[:, c, :], func=ACT.Identity, scale=w_dist, bias=bias
+                        )
+                    else:
+                        nc.gpsimd.tensor_scalar(
+                            out=dist_term[:], in0=dist_all[:, c, :], scalar1=w_dist, scalar2=bias,
+                            op0=ALU.mult, op1=ALU.add,
+                        )
                     node_terms = banks.tile([P, EDGE_CHUNK], F32, tag="bank")
                     nc.tensor.matmul_mx(
                         out=node_terms[:],
@@ -222,7 +228,7 @@ def tile_graphmessagelayer_pa_k_kernel(tc, node_state, positions, We1, be1, We2,
                         start=False,
                         stop=True,
                     )
-                    nc.vector.tensor_tensor(out=pre[:, t, :], in0=node_terms[:], in1=dist_term[:, t, :], op=ALU.add)
+                    nc.vector.tensor_tensor(out=pre[:, t, :], in0=node_terms[:], in1=dist_term[:], op=ALU.add)
 
                 h_bf16 = work.tile([P, EDGE_CHUNK, PACK], BF16, align_bytes=64)
                 nc.scalar.activation(

@@ -28,10 +28,9 @@ HIDDEN_TILES = HIDDEN // P
 J_PER_CHUNK = 4
 EDGE_CHUNK = J_PER_CHUNK * NODES
 EDGE_CHUNKS = NODES_PER_GRAPH // J_PER_CHUNK
-WE1_COLS = 1024
-WE2_PASSES = 4
+WE2_PASSES = 2
 RUN = 4
-SCALAR_PLANE = PACK - 1
+LAST = PACK - 1
 
 SMALLEST_SQUARE = 2.0 ** -100
 
@@ -49,8 +48,8 @@ def tile_graphmessagelayer_pa_k_kernel(tc, node_state, positions, We1, be1, We2,
     nc = tc.nc
     with ExitStack() as ctx:
         keep = ctx.enter_context(tc.tile_pool(name="keep", bufs=1))
-        loads = ctx.enter_context(tc.tile_pool(name="loads", bufs=3))
-        groupeds = ctx.enter_context(tc.tile_pool(name="groupeds", bufs=2))
+        loads = ctx.enter_context(tc.tile_pool(name="loads", bufs=6))
+        groupeds = ctx.enter_context(tc.tile_pool(name="groupeds", bufs=4))
         work = ctx.enter_context(tc.tile_pool(name="work", bufs=2))
         terms = ctx.enter_context(tc.tile_pool(name="terms", bufs=6))
         pres = ctx.enter_context(tc.tile_pool(name="pres", bufs=3))
@@ -120,6 +119,15 @@ def tile_graphmessagelayer_pa_k_kernel(tc, node_state, positions, We1, be1, We2,
         nc.tensor.transpose(out=vecT[:], in_=vec_rows[:], identity=ident_bf16[:])
         vec_cols = keep.tile([P, P], F32)
         nc.vector.tensor_copy(out=vec_cols[:], in_=vecT[:])
+        w_dist = vec_cols[:, 0:HIDDEN_TILES].rearrange("p (g t) -> p g t", t=PACK)
+        be1_cols = vec_cols[:, HIDDEN_TILES:P].rearrange("p (g t) -> p g t", t=PACK)
+        be1_rest = keep.tile([P, HIDDEN_PASSES, PACK], F32)
+        nc.vector.tensor_tensor(
+            out=be1_rest[:],
+            in0=be1_cols,
+            in1=be1_cols[:, :, LAST : LAST + 1].to_broadcast([P, HIDDEN_PASSES, PACK]),
+            op=ALU.subtract,
+        )
 
         rel = keep.tile([P, NODES_PER_GRAPH, COORDS], F32)
         nc.vector.tensor_tensor(
@@ -140,7 +148,7 @@ def tile_graphmessagelayer_pa_k_kernel(tc, node_state, positions, We1, be1, We2,
         nc.vector.scalar_tensor_tensor(
             out=dist[:], in0=sq[:], scalar=0.0, in1=root[:], op0=ALU.is_gt, op1=ALU.mult
         )
-        dist_rep = loads.tile([P, NODES_PER_GRAPH, P], F32, tag="rows")
+        dist_rep = pres.tile([P, NODES_PER_GRAPH, P], F32, tag="pre")
         nc.vector.tensor_copy(out=dist_rep[:], in_=dist[:].unsqueeze(2).to_broadcast([P, NODES_PER_GRAPH, P]))
         dist_all = keep.tile([P, EDGE_CHUNKS, EDGE_CHUNK], F32)
         for c in range(EDGE_CHUNKS):
@@ -157,13 +165,13 @@ def tile_graphmessagelayer_pa_k_kernel(tc, node_state, positions, We1, be1, We2,
         we2_scales = keep.tile([P, HIDDEN_PASSES, MESSAGE], U8, align_bytes=64)
         we2_view = We2.rearrange("(g t p) m -> p g t m", t=PACK, p=P)
 
-        def quantise_we1(first_col):
-            cols = slice(first_col, first_col + WE1_COLS)
+        def quantise_we1(g):
+            cols = slice(g * K_PASS, (g + 1) * K_PASS)
             for blk, copy in ((0, nc.vector.tensor_copy), (1, nc.scalar.copy)):
-                rows = loads.tile([P, PACK, WE1_COLS], BF16, tag="rows")
+                rows = loads.tile([P, PACK, K_PASS], BF16, tag="rows")
                 block = We1[blk * FEATURES : (blk + 1) * FEATURES, :].rearrange("(t p) f -> p t f", p=P)
                 nc.sync.dma_start(out=rows[:], in_=block[:, :, cols])
-                grouped = groupeds.tile([P, WE1_COLS, PACK], BF16, tag="grouped", align_bytes=64)
+                grouped = groupeds.tile([P, K_PASS, PACK], BF16, tag="grouped", align_bytes=64)
                 regroup(copy, grouped[:], rows[:])
                 nc.vector.quantize_mx(
                     out=we1_codes[blk][:, cols].bitcast(FP8X4),
@@ -184,31 +192,23 @@ def tile_graphmessagelayer_pa_k_kernel(tc, node_state, positions, We1, be1, We2,
                 in_=grouped[:].rearrange("p g m t -> p (g m t)"),
             )
 
+        def prepare_weights(g):
+            quantise_we1(g)
+            if g % WE2_PASSES == 0:
+                quantise_we2(g)
+
         out_rows = out.rearrange("b i j m -> (b i) j m")
+        prepare_weights(0)
         for c in range(EDGE_CHUNKS):
             msg = [sums.tile([P, MESSAGE], F32, name="msg%d" % s) for s in range(J_PER_CHUNK)]
             for g in range(HIDDEN_PASSES):
-                if c == 0 and (g * K_PASS) % WE1_COLS == 0:
-                    quantise_we1(g * K_PASS)
-                if c == 0 and g % WE2_PASSES == 0:
-                    quantise_we2(g)
+                if c == 0 and g + 1 < HIDDEN_PASSES:
+                    prepare_weights(g + 1)
 
                 pre = pres.tile([P, PACK, EDGE_CHUNK], F32)
                 for t in range(PACK):
                     q = g * PACK + t
                     f_cols = slice(q * P, (q + 1) * P)
-                    dist_term = terms.tile([P, EDGE_CHUNK], F32)
-                    w_dist = vec_cols[:, q : q + 1]
-                    bias = vec_cols[:, HIDDEN_TILES + q : HIDDEN_TILES + q + 1]
-                    if t == SCALAR_PLANE:
-                        nc.scalar.activation(
-                            out=dist_term[:], in_=dist_all[:, c, :], func=ACT.Identity, scale=w_dist, bias=bias
-                        )
-                    else:
-                        nc.gpsimd.tensor_scalar(
-                            out=dist_term[:], in0=dist_all[:, c, :], scalar1=w_dist, scalar2=bias,
-                            op0=ALU.mult, op1=ALU.add,
-                        )
                     node_terms = banks.tile([P, EDGE_CHUNK], F32, tag="bank")
                     nc.tensor.matmul_mx(
                         out=node_terms[:],
@@ -228,13 +228,25 @@ def tile_graphmessagelayer_pa_k_kernel(tc, node_state, positions, We1, be1, We2,
                         start=False,
                         stop=True,
                     )
-                    nc.vector.tensor_tensor(out=pre[:, t, :], in0=node_terms[:], in1=dist_term[:], op=ALU.add)
+                    if t == LAST:
+                        nc.vector.scalar_tensor_tensor(
+                            out=pre[:, t, :], in0=dist_all[:, c, :], scalar=w_dist[:, g, t : t + 1],
+                            in1=node_terms[:], op0=ALU.mult, op1=ALU.add,
+                        )
+                    else:
+                        dist_term = terms.tile([P, EDGE_CHUNK], F32)
+                        nc.gpsimd.tensor_scalar(
+                            out=dist_term[:], in0=dist_all[:, c, :], scalar1=w_dist[:, g, t : t + 1],
+                            scalar2=be1_rest[:, g, t : t + 1], op0=ALU.mult, op1=ALU.add,
+                        )
+                        nc.vector.tensor_tensor(out=pre[:, t, :], in0=node_terms[:], in1=dist_term[:], op=ALU.add)
 
                 h_bf16 = work.tile([P, EDGE_CHUNK, PACK], BF16, align_bytes=64)
                 nc.scalar.activation(
                     out=h_bf16[:].rearrange("p (c i) t -> p c t i", i=RUN),
                     in_=pre[:].rearrange("p t (c i) -> p c t i", i=RUN),
                     func=ACT.Silu,
+                    bias=be1_cols[:, g, LAST : LAST + 1],
                 )
                 h_codes = work.tile([P, EDGE_CHUNK], U32, align_bytes=64)
                 h_scales = work.tile([P, EDGE_CHUNK], U8, align_bytes=64)

@@ -28,7 +28,10 @@ HIDDEN_TILES = HIDDEN // P
 J_PER_CHUNK = 4
 EDGE_CHUNK = J_PER_CHUNK * NODES
 EDGE_CHUNKS = NODES_PER_GRAPH // J_PER_CHUNK
-WE2_PASSES = 2
+WE2_LOAD = 2
+WE2_PASSES = 4
+H_PASSES = 2
+BLOCKS = 2
 RUN = 4
 LAST = PACK - 1
 
@@ -48,8 +51,8 @@ def tile_graphmessagelayer_pa_k_kernel(tc, node_state, positions, We1, be1, We2,
     nc = tc.nc
     with ExitStack() as ctx:
         keep = ctx.enter_context(tc.tile_pool(name="keep", bufs=1))
-        loads = ctx.enter_context(tc.tile_pool(name="loads", bufs=6))
-        groupeds = ctx.enter_context(tc.tile_pool(name="groupeds", bufs=4))
+        loads = ctx.enter_context(tc.tile_pool(name="loads", bufs=4))
+        groupeds = ctx.enter_context(tc.tile_pool(name="groupeds", bufs=2))
         work = ctx.enter_context(tc.tile_pool(name="work", bufs=2))
         terms = ctx.enter_context(tc.tile_pool(name="terms", bufs=6))
         pres = ctx.enter_context(tc.tile_pool(name="pres", bufs=3))
@@ -159,33 +162,36 @@ def tile_graphmessagelayer_pa_k_kernel(tc, node_state, positions, We1, be1, We2,
                 )
             nc.scalar.copy(out=dist_all[:, c, :], in_=distT[:].rearrange("p s n -> p (s n)"))
 
-        we1_codes = [keep.tile([P, HIDDEN], U32, name="we1_codes%d" % blk, align_bytes=64) for blk in range(2)]
-        we1_scales = [keep.tile([P, HIDDEN], U8, name="we1_scales%d" % blk, align_bytes=64) for blk in range(2)]
+        we1_codes = keep.tile([P, HIDDEN_PASSES, BLOCKS, K_PASS], U32, align_bytes=64)
+        we1_scales = keep.tile([P, HIDDEN_PASSES, BLOCKS, K_PASS], U8, align_bytes=64)
         we2_codes = keep.tile([P, HIDDEN_PASSES, MESSAGE], U32, align_bytes=64)
         we2_scales = keep.tile([P, HIDDEN_PASSES, MESSAGE], U8, align_bytes=64)
         we2_view = We2.rearrange("(g t p) m -> p g t m", t=PACK, p=P)
 
         def quantise_we1(g):
             cols = slice(g * K_PASS, (g + 1) * K_PASS)
+            grouped = groupeds.tile([P, BLOCKS, K_PASS, PACK], BF16, tag="grouped", align_bytes=64)
             for blk, copy in ((0, nc.vector.tensor_copy), (1, nc.scalar.copy)):
                 rows = loads.tile([P, PACK, K_PASS], BF16, tag="rows")
                 block = We1[blk * FEATURES : (blk + 1) * FEATURES, :].rearrange("(t p) f -> p t f", p=P)
                 nc.sync.dma_start(out=rows[:], in_=block[:, :, cols])
-                grouped = groupeds.tile([P, K_PASS, PACK], BF16, tag="grouped", align_bytes=64)
-                regroup(copy, grouped[:], rows[:])
-                nc.vector.quantize_mx(
-                    out=we1_codes[blk][:, cols].bitcast(FP8X4),
-                    scales=we1_scales[blk][:, cols],
-                    in_=grouped[:].rearrange("p f t -> p (f t)"),
-                )
+                regroup(copy, grouped[:, blk], rows[:])
+            nc.vector.quantize_mx(
+                out=we1_codes[:, g].rearrange("p k f -> p (k f)").bitcast(FP8X4),
+                scales=we1_scales[:, g].rearrange("p k f -> p (k f)"),
+                in_=grouped[:].rearrange("p k f t -> p (k f t)"),
+            )
 
         def quantise_we2(first_pass):
             passes = slice(first_pass, first_pass + WE2_PASSES)
-            rows = loads.tile([P, WE2_PASSES, PACK, MESSAGE], BF16, tag="rows")
-            nc.sync.dma_start(out=rows[:], in_=we2_view[:, passes])
             grouped = groupeds.tile([P, WE2_PASSES, MESSAGE, PACK], BF16, tag="grouped", align_bytes=64)
-            for g in range(WE2_PASSES):
-                regroup(nc.scalar.copy, grouped[:, g], rows[:, g])
+            for first in range(0, WE2_PASSES, WE2_LOAD):
+                rows = loads.tile([P, WE2_LOAD, PACK, MESSAGE], BF16, tag="rows")
+                nc.sync.dma_start(
+                    out=rows[:], in_=we2_view[:, first_pass + first : first_pass + first + WE2_LOAD]
+                )
+                for k in range(WE2_LOAD):
+                    regroup(nc.scalar.copy, grouped[:, first + k], rows[:, k])
             nc.vector.quantize_mx(
                 out=we2_codes[:, passes, :].rearrange("p g m -> p (g m)").bitcast(FP8X4),
                 scales=we2_scales[:, passes, :].rearrange("p g m -> p (g m)"),
@@ -201,71 +207,77 @@ def tile_graphmessagelayer_pa_k_kernel(tc, node_state, positions, We1, be1, We2,
         prepare_weights(0)
         for c in range(EDGE_CHUNKS):
             msg = [sums.tile([P, MESSAGE], F32, name="msg%d" % s) for s in range(J_PER_CHUNK)]
-            for g in range(HIDDEN_PASSES):
-                if c == 0 and g + 1 < HIDDEN_PASSES:
-                    prepare_weights(g + 1)
+            for first_pass in range(0, HIDDEN_PASSES, H_PASSES):
+                h_bf16 = work.tile([P, H_PASSES, EDGE_CHUNK, PACK], BF16, align_bytes=64)
+                for k in range(H_PASSES):
+                    g = first_pass + k
+                    if c == 0 and g + 1 < HIDDEN_PASSES:
+                        prepare_weights(g + 1)
 
-                pre = pres.tile([P, PACK, EDGE_CHUNK], F32)
-                for t in range(PACK):
-                    q = g * PACK + t
-                    f_cols = slice(q * P, (q + 1) * P)
-                    node_terms = banks.tile([P, EDGE_CHUNK], F32, tag="bank")
-                    nc.tensor.matmul_mx(
-                        out=node_terms[:],
-                        lhsT=we1_codes[0][:, f_cols].bitcast(FP8X4),
-                        lhsT_scale=we1_scales[0][:, f_cols],
-                        rhs=xi_codes[:].bitcast(FP8X4),
-                        rhs_scale=xi_scales[:],
-                        start=True,
-                        stop=False,
-                    )
-                    nc.tensor.matmul_mx(
-                        out=node_terms[:],
-                        lhsT=we1_codes[1][:, f_cols].bitcast(FP8X4),
-                        lhsT_scale=we1_scales[1][:, f_cols],
-                        rhs=xj_codes[:, c, :].bitcast(FP8X4),
-                        rhs_scale=xj_scales[:, c, :],
-                        start=False,
-                        stop=True,
-                    )
-                    if t == LAST:
-                        nc.vector.scalar_tensor_tensor(
-                            out=pre[:, t, :], in0=dist_all[:, c, :], scalar=w_dist[:, g, t : t + 1],
-                            in1=node_terms[:], op0=ALU.mult, op1=ALU.add,
+                    pre = pres.tile([P, PACK, EDGE_CHUNK], F32)
+                    for t in range(PACK):
+                        f_cols = slice(t * P, (t + 1) * P)
+                        node_terms = banks.tile([P, EDGE_CHUNK], F32, tag="bank")
+                        nc.tensor.matmul_mx(
+                            out=node_terms[:],
+                            lhsT=we1_codes[:, g, 0, f_cols].bitcast(FP8X4),
+                            lhsT_scale=we1_scales[:, g, 0, f_cols],
+                            rhs=xi_codes[:].bitcast(FP8X4),
+                            rhs_scale=xi_scales[:],
+                            start=True,
+                            stop=False,
                         )
-                    else:
-                        dist_term = terms.tile([P, EDGE_CHUNK], F32)
-                        nc.gpsimd.tensor_scalar(
-                            out=dist_term[:], in0=dist_all[:, c, :], scalar1=w_dist[:, g, t : t + 1],
-                            scalar2=be1_rest[:, g, t : t + 1], op0=ALU.mult, op1=ALU.add,
+                        nc.tensor.matmul_mx(
+                            out=node_terms[:],
+                            lhsT=we1_codes[:, g, 1, f_cols].bitcast(FP8X4),
+                            lhsT_scale=we1_scales[:, g, 1, f_cols],
+                            rhs=xj_codes[:, c, :].bitcast(FP8X4),
+                            rhs_scale=xj_scales[:, c, :],
+                            start=False,
+                            stop=True,
                         )
-                        nc.vector.tensor_tensor(out=pre[:, t, :], in0=node_terms[:], in1=dist_term[:], op=ALU.add)
+                        if t == LAST:
+                            nc.vector.scalar_tensor_tensor(
+                                out=pre[:, t, :], in0=dist_all[:, c, :], scalar=w_dist[:, g, t : t + 1],
+                                in1=node_terms[:], op0=ALU.mult, op1=ALU.add,
+                            )
+                        else:
+                            dist_term = terms.tile([P, EDGE_CHUNK], F32)
+                            nc.gpsimd.tensor_scalar(
+                                out=dist_term[:], in0=dist_all[:, c, :], scalar1=w_dist[:, g, t : t + 1],
+                                scalar2=be1_rest[:, g, t : t + 1], op0=ALU.mult, op1=ALU.add,
+                            )
+                            nc.vector.tensor_tensor(
+                                out=pre[:, t, :], in0=node_terms[:], in1=dist_term[:], op=ALU.add
+                            )
 
-                h_bf16 = work.tile([P, EDGE_CHUNK, PACK], BF16, align_bytes=64)
-                nc.scalar.activation(
-                    out=h_bf16[:].rearrange("p (c i) t -> p c t i", i=RUN),
-                    in_=pre[:].rearrange("p t (c i) -> p c t i", i=RUN),
-                    func=ACT.Silu,
-                    bias=be1_cols[:, g, LAST : LAST + 1],
-                )
-                h_codes = work.tile([P, EDGE_CHUNK], U32, align_bytes=64)
-                h_scales = work.tile([P, EDGE_CHUNK], U8, align_bytes=64)
+                    nc.scalar.activation(
+                        out=h_bf16[:, k].rearrange("p (c i) t -> p c t i", i=RUN),
+                        in_=pre[:].rearrange("p t (c i) -> p c t i", i=RUN),
+                        func=ACT.Silu,
+                        bias=be1_cols[:, g, LAST : LAST + 1],
+                    )
+
+                h_codes = work.tile([P, H_PASSES, EDGE_CHUNK], U32, align_bytes=64)
+                h_scales = work.tile([P, H_PASSES, EDGE_CHUNK], U8, align_bytes=64)
                 nc.vector.quantize_mx(
-                    out=h_codes[:].bitcast(FP8X4),
-                    scales=h_scales[:],
-                    in_=h_bf16[:].rearrange("p e t -> p (e t)"),
+                    out=h_codes[:].rearrange("p k e -> p (k e)").bitcast(FP8X4),
+                    scales=h_scales[:].rearrange("p k e -> p (k e)"),
+                    in_=h_bf16[:].rearrange("p k e t -> p (k e t)"),
                 )
-                for s in range(J_PER_CHUNK):
-                    e_cols = slice(s * NODES, (s + 1) * NODES)
-                    nc.tensor.matmul_mx(
-                        out=msg[s][:],
-                        lhsT=h_codes[:, e_cols].bitcast(FP8X4),
-                        lhsT_scale=h_scales[:, e_cols],
-                        rhs=we2_codes[:, g, :].bitcast(FP8X4),
-                        rhs_scale=we2_scales[:, g, :],
-                        start=(g == 0),
-                        stop=(g == HIDDEN_PASSES - 1),
-                    )
+                for k in range(H_PASSES):
+                    g = first_pass + k
+                    for s in range(J_PER_CHUNK):
+                        e_cols = slice(s * NODES, (s + 1) * NODES)
+                        nc.tensor.matmul_mx(
+                            out=msg[s][:],
+                            lhsT=h_codes[:, k, e_cols].bitcast(FP8X4),
+                            lhsT_scale=h_scales[:, k, e_cols],
+                            rhs=we2_codes[:, g, :].bitcast(FP8X4),
+                            rhs_scale=we2_scales[:, g, :],
+                            start=(g == 0),
+                            stop=(g == HIDDEN_PASSES - 1),
+                        )
 
             result = work.tile([P, J_PER_CHUNK, MESSAGE], F32)
             for s in range(J_PER_CHUNK):

@@ -28,12 +28,10 @@ HIDDEN_TILES = HIDDEN // P
 J_PER_CHUNK = 4
 EDGE_CHUNK = J_PER_CHUNK * NODES
 EDGE_CHUNKS = NODES_PER_GRAPH // J_PER_CHUNK
-WE2_LOAD = 2
-WE2_PASSES = 4
-H_PASSES = 2
-BLOCKS = 2
+WE2_PASSES = 2
 RUN = 4
 LAST = PACK - 1
+SHARED = PACK - 2
 
 SMALLEST_SQUARE = 2.0 ** -100
 
@@ -51,8 +49,8 @@ def tile_graphmessagelayer_pa_k_kernel(tc, node_state, positions, We1, be1, We2,
     nc = tc.nc
     with ExitStack() as ctx:
         keep = ctx.enter_context(tc.tile_pool(name="keep", bufs=1))
-        loads = ctx.enter_context(tc.tile_pool(name="loads", bufs=4))
-        groupeds = ctx.enter_context(tc.tile_pool(name="groupeds", bufs=2))
+        loads = ctx.enter_context(tc.tile_pool(name="loads", bufs=6))
+        groupeds = ctx.enter_context(tc.tile_pool(name="groupeds", bufs=4))
         work = ctx.enter_context(tc.tile_pool(name="work", bufs=2))
         terms = ctx.enter_context(tc.tile_pool(name="terms", bufs=6))
         pres = ctx.enter_context(tc.tile_pool(name="pres", bufs=3))
@@ -162,36 +160,33 @@ def tile_graphmessagelayer_pa_k_kernel(tc, node_state, positions, We1, be1, We2,
                 )
             nc.scalar.copy(out=dist_all[:, c, :], in_=distT[:].rearrange("p s n -> p (s n)"))
 
-        we1_codes = keep.tile([P, HIDDEN_PASSES, BLOCKS, K_PASS], U32, align_bytes=64)
-        we1_scales = keep.tile([P, HIDDEN_PASSES, BLOCKS, K_PASS], U8, align_bytes=64)
+        we1_codes = [keep.tile([P, HIDDEN], U32, name="we1_codes%d" % blk, align_bytes=64) for blk in range(2)]
+        we1_scales = [keep.tile([P, HIDDEN], U8, name="we1_scales%d" % blk, align_bytes=64) for blk in range(2)]
         we2_codes = keep.tile([P, HIDDEN_PASSES, MESSAGE], U32, align_bytes=64)
         we2_scales = keep.tile([P, HIDDEN_PASSES, MESSAGE], U8, align_bytes=64)
         we2_view = We2.rearrange("(g t p) m -> p g t m", t=PACK, p=P)
 
         def quantise_we1(g):
             cols = slice(g * K_PASS, (g + 1) * K_PASS)
-            grouped = groupeds.tile([P, BLOCKS, K_PASS, PACK], BF16, tag="grouped", align_bytes=64)
             for blk, copy in ((0, nc.vector.tensor_copy), (1, nc.scalar.copy)):
                 rows = loads.tile([P, PACK, K_PASS], BF16, tag="rows")
                 block = We1[blk * FEATURES : (blk + 1) * FEATURES, :].rearrange("(t p) f -> p t f", p=P)
                 nc.sync.dma_start(out=rows[:], in_=block[:, :, cols])
-                regroup(copy, grouped[:, blk], rows[:])
-            nc.vector.quantize_mx(
-                out=we1_codes[:, g].rearrange("p k f -> p (k f)").bitcast(FP8X4),
-                scales=we1_scales[:, g].rearrange("p k f -> p (k f)"),
-                in_=grouped[:].rearrange("p k f t -> p (k f t)"),
-            )
+                grouped = groupeds.tile([P, K_PASS, PACK], BF16, tag="grouped", align_bytes=64)
+                regroup(copy, grouped[:], rows[:])
+                nc.vector.quantize_mx(
+                    out=we1_codes[blk][:, cols].bitcast(FP8X4),
+                    scales=we1_scales[blk][:, cols],
+                    in_=grouped[:].rearrange("p f t -> p (f t)"),
+                )
 
         def quantise_we2(first_pass):
             passes = slice(first_pass, first_pass + WE2_PASSES)
+            rows = loads.tile([P, WE2_PASSES, PACK, MESSAGE], BF16, tag="rows")
+            nc.sync.dma_start(out=rows[:], in_=we2_view[:, passes])
             grouped = groupeds.tile([P, WE2_PASSES, MESSAGE, PACK], BF16, tag="grouped", align_bytes=64)
-            for first in range(0, WE2_PASSES, WE2_LOAD):
-                rows = loads.tile([P, WE2_LOAD, PACK, MESSAGE], BF16, tag="rows")
-                nc.sync.dma_start(
-                    out=rows[:], in_=we2_view[:, first_pass + first : first_pass + first + WE2_LOAD]
-                )
-                for k in range(WE2_LOAD):
-                    regroup(nc.scalar.copy, grouped[:, first + k], rows[:, k])
+            for g in range(WE2_PASSES):
+                regroup(nc.scalar.copy, grouped[:, g], rows[:, g])
             nc.vector.quantize_mx(
                 out=we2_codes[:, passes, :].rearrange("p g m -> p (g m)").bitcast(FP8X4),
                 scales=we2_scales[:, passes, :].rearrange("p g m -> p (g m)"),
@@ -207,77 +202,77 @@ def tile_graphmessagelayer_pa_k_kernel(tc, node_state, positions, We1, be1, We2,
         prepare_weights(0)
         for c in range(EDGE_CHUNKS):
             msg = [sums.tile([P, MESSAGE], F32, name="msg%d" % s) for s in range(J_PER_CHUNK)]
-            for first_pass in range(0, HIDDEN_PASSES, H_PASSES):
-                h_bf16 = work.tile([P, H_PASSES, EDGE_CHUNK, PACK], BF16, align_bytes=64)
-                for k in range(H_PASSES):
-                    g = first_pass + k
-                    if c == 0 and g + 1 < HIDDEN_PASSES:
-                        prepare_weights(g + 1)
+            for g in range(HIDDEN_PASSES):
+                if c == 0 and g + 1 < HIDDEN_PASSES:
+                    prepare_weights(g + 1)
 
-                    pre = pres.tile([P, PACK, EDGE_CHUNK], F32)
-                    for t in range(PACK):
-                        f_cols = slice(t * P, (t + 1) * P)
-                        node_terms = banks.tile([P, EDGE_CHUNK], F32, tag="bank")
-                        nc.tensor.matmul_mx(
-                            out=node_terms[:],
-                            lhsT=we1_codes[:, g, 0, f_cols].bitcast(FP8X4),
-                            lhsT_scale=we1_scales[:, g, 0, f_cols],
-                            rhs=xi_codes[:].bitcast(FP8X4),
-                            rhs_scale=xi_scales[:],
-                            start=True,
-                            stop=False,
+                pre = pres.tile([P, PACK, EDGE_CHUNK], F32)
+                for t in range(PACK):
+                    q = g * PACK + t
+                    f_cols = slice(q * P, (q + 1) * P)
+                    node_terms = banks.tile([P, EDGE_CHUNK], F32, tag="bank")
+                    nc.tensor.matmul_mx(
+                        out=node_terms[:],
+                        lhsT=we1_codes[0][:, f_cols].bitcast(FP8X4),
+                        lhsT_scale=we1_scales[0][:, f_cols],
+                        rhs=xi_codes[:].bitcast(FP8X4),
+                        rhs_scale=xi_scales[:],
+                        start=True,
+                        stop=False,
+                    )
+                    nc.tensor.matmul_mx(
+                        out=node_terms[:],
+                        lhsT=we1_codes[1][:, f_cols].bitcast(FP8X4),
+                        lhsT_scale=we1_scales[1][:, f_cols],
+                        rhs=xj_codes[:, c, :].bitcast(FP8X4),
+                        rhs_scale=xj_scales[:, c, :],
+                        start=False,
+                        stop=True,
+                    )
+                    if t == LAST:
+                        nc.vector.scalar_tensor_tensor(
+                            out=pre[:, t, :], in0=dist_all[:, c, :], scalar=w_dist[:, g, t : t + 1],
+                            in1=node_terms[:], op0=ALU.mult, op1=ALU.add,
                         )
-                        nc.tensor.matmul_mx(
-                            out=node_terms[:],
-                            lhsT=we1_codes[:, g, 1, f_cols].bitcast(FP8X4),
-                            lhsT_scale=we1_scales[:, g, 1, f_cols],
-                            rhs=xj_codes[:, c, :].bitcast(FP8X4),
-                            rhs_scale=xj_scales[:, c, :],
-                            start=False,
-                            stop=True,
-                        )
-                        if t == LAST:
-                            nc.vector.scalar_tensor_tensor(
-                                out=pre[:, t, :], in0=dist_all[:, c, :], scalar=w_dist[:, g, t : t + 1],
-                                in1=node_terms[:], op0=ALU.mult, op1=ALU.add,
+                    else:
+                        dist_term = terms.tile([P, EDGE_CHUNK], F32)
+                        if t == SHARED and g % 2 == 1:
+                            nc.scalar.activation(
+                                out=dist_term[:], in_=dist_all[:, c, :], func=ACT.Identity,
+                                scale=w_dist[:, g, t : t + 1], bias=be1_rest[:, g, t : t + 1],
                             )
                         else:
-                            dist_term = terms.tile([P, EDGE_CHUNK], F32)
                             nc.gpsimd.tensor_scalar(
                                 out=dist_term[:], in0=dist_all[:, c, :], scalar1=w_dist[:, g, t : t + 1],
                                 scalar2=be1_rest[:, g, t : t + 1], op0=ALU.mult, op1=ALU.add,
                             )
-                            nc.vector.tensor_tensor(
-                                out=pre[:, t, :], in0=node_terms[:], in1=dist_term[:], op=ALU.add
-                            )
+                        nc.vector.tensor_tensor(out=pre[:, t, :], in0=node_terms[:], in1=dist_term[:], op=ALU.add)
 
-                    nc.scalar.activation(
-                        out=h_bf16[:, k].rearrange("p (c i) t -> p c t i", i=RUN),
-                        in_=pre[:].rearrange("p t (c i) -> p c t i", i=RUN),
-                        func=ACT.Silu,
-                        bias=be1_cols[:, g, LAST : LAST + 1],
-                    )
-
-                h_codes = work.tile([P, H_PASSES, EDGE_CHUNK], U32, align_bytes=64)
-                h_scales = work.tile([P, H_PASSES, EDGE_CHUNK], U8, align_bytes=64)
-                nc.vector.quantize_mx(
-                    out=h_codes[:].rearrange("p k e -> p (k e)").bitcast(FP8X4),
-                    scales=h_scales[:].rearrange("p k e -> p (k e)"),
-                    in_=h_bf16[:].rearrange("p k e t -> p (k e t)"),
+                h_bf16 = work.tile([P, EDGE_CHUNK, PACK], BF16, align_bytes=64)
+                nc.scalar.activation(
+                    out=h_bf16[:].rearrange("p (c i) t -> p c t i", i=RUN),
+                    in_=pre[:].rearrange("p t (c i) -> p c t i", i=RUN),
+                    func=ACT.Silu,
+                    bias=be1_cols[:, g, LAST : LAST + 1],
                 )
-                for k in range(H_PASSES):
-                    g = first_pass + k
-                    for s in range(J_PER_CHUNK):
-                        e_cols = slice(s * NODES, (s + 1) * NODES)
-                        nc.tensor.matmul_mx(
-                            out=msg[s][:],
-                            lhsT=h_codes[:, k, e_cols].bitcast(FP8X4),
-                            lhsT_scale=h_scales[:, k, e_cols],
-                            rhs=we2_codes[:, g, :].bitcast(FP8X4),
-                            rhs_scale=we2_scales[:, g, :],
-                            start=(g == 0),
-                            stop=(g == HIDDEN_PASSES - 1),
-                        )
+                h_codes = work.tile([P, EDGE_CHUNK], U32, align_bytes=64)
+                h_scales = work.tile([P, EDGE_CHUNK], U8, align_bytes=64)
+                nc.vector.quantize_mx(
+                    out=h_codes[:].bitcast(FP8X4),
+                    scales=h_scales[:],
+                    in_=h_bf16[:].rearrange("p e t -> p (e t)"),
+                )
+                for s in range(J_PER_CHUNK):
+                    e_cols = slice(s * NODES, (s + 1) * NODES)
+                    nc.tensor.matmul_mx(
+                        out=msg[s][:],
+                        lhsT=h_codes[:, e_cols].bitcast(FP8X4),
+                        lhsT_scale=h_scales[:, e_cols],
+                        rhs=we2_codes[:, g, :].bitcast(FP8X4),
+                        rhs_scale=we2_scales[:, g, :],
+                        start=(g == 0),
+                        stop=(g == HIDDEN_PASSES - 1),
+                    )
 
             result = work.tile([P, J_PER_CHUNK, MESSAGE], F32)
             for s in range(J_PER_CHUNK):

@@ -30,6 +30,7 @@ EDGE_CHUNK = J_PER_CHUNK * NODES
 EDGE_CHUNKS = NODES_PER_GRAPH // J_PER_CHUNK
 WE2_PASSES = 2
 RUN = 4
+WEIGHT_RUN = 8
 LAST = PACK - 1
 SHARED = PACK - 2
 
@@ -40,8 +41,8 @@ FLOPS = 2 * NODES * 2 * FEATURES * HIDDEN + 2 * NODES * NODES_PER_GRAPH * HIDDEN
 
 def regroup(copy, grouped, rows):
     copy(
-        out=grouped.rearrange("p (c i) t -> p c t i", i=RUN),
-        in_=rows.rearrange("p t (c i) -> p c t i", i=RUN),
+        out=grouped.rearrange("p (c i) t -> p c t i", i=WEIGHT_RUN),
+        in_=rows.rearrange("p t (c i) -> p c t i", i=WEIGHT_RUN),
     )
 
 

@@ -54,7 +54,7 @@ def tile_graphmessagelayer_pa_k_kernel(tc, node_state, positions, We1, be1, We2,
         groupeds = ctx.enter_context(tc.tile_pool(name="groupeds", bufs=4))
         work = ctx.enter_context(tc.tile_pool(name="work", bufs=2))
         terms = ctx.enter_context(tc.tile_pool(name="terms", bufs=6))
-        pres = ctx.enter_context(tc.tile_pool(name="pres", bufs=3))
+        pres = ctx.enter_context(tc.tile_pool(name="pres", bufs=4))
         banks = ctx.enter_context(tc.psum_pool(name="banks", bufs=4))
         sums = ctx.enter_context(tc.psum_pool(name="sums", bufs=1))
 
@@ -88,23 +88,23 @@ def tile_graphmessagelayer_pa_k_kernel(tc, node_state, positions, We1, be1, We2,
         x_words = keep.tile([P, NODES, PACK], BF16)
         nc.vector.tensor_copy(out=x_words[:], in_=xT[:].rearrange("p t n -> p n t"))
 
-        xi_in = work.tile([P, J_PER_CHUNK, NODES, PACK], BF16, tag="h_bf16", align_bytes=64)
+        xi_in = work.tile([P, J_PER_CHUNK, NODES, PACK], BF16, tag="h_bf16", bufs=3, align_bytes=64)
         nc.vector.tensor_copy(
             out=xi_in[:], in_=x_words[:].unsqueeze(1).to_broadcast([P, J_PER_CHUNK, NODES, PACK])
         )
-        xi_codes = keep.tile([P, EDGE_CHUNK], U32, align_bytes=64)
-        xi_scales = keep.tile([P, EDGE_CHUNK], U8, align_bytes=64)
+        xi_codes = keep.tile([P, EDGE_CHUNK], U32, align_bytes=256)
+        xi_scales = keep.tile([P, EDGE_CHUNK], U8, align_bytes=256)
         nc.vector.quantize_mx(
             out=xi_codes[:].bitcast(FP8X4),
             scales=xi_scales[:],
             in_=xi_in[:].rearrange("p s n t -> p (s n t)"),
         )
 
-        xj_codes = keep.tile([P, EDGE_CHUNKS, EDGE_CHUNK], U32, align_bytes=64)
-        xj_scales = keep.tile([P, EDGE_CHUNKS, EDGE_CHUNK], U8, align_bytes=64)
+        xj_codes = keep.tile([P, EDGE_CHUNKS, EDGE_CHUNK], U32, align_bytes=256)
+        xj_scales = keep.tile([P, EDGE_CHUNKS, EDGE_CHUNK], U8, align_bytes=256)
         x_by_graph = x_words[:].rearrange("p (b n) t -> p b n t", n=NODES_PER_GRAPH)
         for c in range(EDGE_CHUNKS):
-            xj_in = work.tile([P, J_PER_CHUNK, GRAPHS, NODES_PER_GRAPH, PACK], BF16, tag="h_bf16", align_bytes=64)
+            xj_in = work.tile([P, J_PER_CHUNK, GRAPHS, NODES_PER_GRAPH, PACK], BF16, tag="h_bf16", bufs=3, align_bytes=64)
             for s in range(J_PER_CHUNK):
                 j = c * J_PER_CHUNK + s
                 nc.vector.tensor_copy(
@@ -161,10 +161,10 @@ def tile_graphmessagelayer_pa_k_kernel(tc, node_state, positions, We1, be1, We2,
                 )
             nc.scalar.copy(out=dist_all[:, c, :], in_=distT[:].rearrange("p s n -> p (s n)"))
 
-        we1_codes = [keep.tile([P, HIDDEN], U32, name="we1_codes%d" % blk, align_bytes=64) for blk in range(2)]
-        we1_scales = [keep.tile([P, HIDDEN], U8, name="we1_scales%d" % blk, align_bytes=64) for blk in range(2)]
-        we2_codes = keep.tile([P, HIDDEN_PASSES, MESSAGE], U32, align_bytes=64)
-        we2_scales = keep.tile([P, HIDDEN_PASSES, MESSAGE], U8, align_bytes=64)
+        we1_codes = [keep.tile([P, HIDDEN], U32, name="we1_codes%d" % blk, align_bytes=256) for blk in range(2)]
+        we1_scales = [keep.tile([P, HIDDEN], U8, name="we1_scales%d" % blk, align_bytes=256) for blk in range(2)]
+        we2_codes = keep.tile([P, HIDDEN_PASSES, MESSAGE], U32, align_bytes=256)
+        we2_scales = keep.tile([P, HIDDEN_PASSES, MESSAGE], U8, align_bytes=256)
         we2_view = We2.rearrange("(g t p) m -> p g t m", t=PACK, p=P)
 
         def quantise_we1(g):
@@ -249,15 +249,15 @@ def tile_graphmessagelayer_pa_k_kernel(tc, node_state, positions, We1, be1, We2,
                             )
                         nc.vector.tensor_tensor(out=pre[:, t, :], in0=node_terms[:], in1=dist_term[:], op=ALU.add)
 
-                h_bf16 = work.tile([P, EDGE_CHUNK, PACK], BF16, align_bytes=64)
+                h_bf16 = work.tile([P, EDGE_CHUNK, PACK], BF16, bufs=3, align_bytes=64)
                 nc.scalar.activation(
                     out=h_bf16[:].rearrange("p (c i) t -> p c t i", i=RUN),
                     in_=pre[:].rearrange("p t (c i) -> p c t i", i=RUN),
                     func=ACT.Silu,
                     bias=be1_cols[:, g, LAST : LAST + 1],
                 )
-                h_codes = work.tile([P, EDGE_CHUNK], U32, align_bytes=64)
-                h_scales = work.tile([P, EDGE_CHUNK], U8, align_bytes=64)
+                h_codes = work.tile([P, EDGE_CHUNK], U32, bufs=3, align_bytes=256)
+                h_scales = work.tile([P, EDGE_CHUNK], U8, bufs=3, align_bytes=256)
                 nc.vector.quantize_mx(
                     out=h_codes[:].bitcast(FP8X4),
                     scales=h_scales[:],

from contextlib import ExitStack

import concourse.mybir as mybir
from concourse.masks import make_identity

F32 = mybir.dt.float32
BF16 = mybir.dt.bfloat16
U32 = mybir.dt.uint32
U8 = mybir.dt.uint8
FP8X4 = mybir.dt.float8_e4m3fn_x4
ALU = mybir.AluOpType
ACT = mybir.ActivationFunctionType

P = 128
PACK = 4
K_PASS = P * PACK

GRAPHS = 8
NODES_PER_GRAPH = 16
NODES = GRAPHS * NODES_PER_GRAPH
COORDS = 3
FEATURES = 512
HIDDEN = 8192
MESSAGE = 256

HIDDEN_PASSES = HIDDEN // K_PASS
HIDDEN_TILES = HIDDEN // P
J_PER_CHUNK = 4
EDGE_CHUNK = J_PER_CHUNK * NODES
EDGE_CHUNKS = NODES_PER_GRAPH // J_PER_CHUNK
WE2_PASSES = 2
RUN = 4
WEIGHT_RUN = 8
LAST = PACK - 1
SHARED = PACK - 2

SMALLEST_SQUARE = 2.0 ** -100

FLOPS = 2 * NODES * 2 * FEATURES * HIDDEN + 2 * NODES * NODES_PER_GRAPH * HIDDEN * MESSAGE


def regroup(copy, grouped, rows):
    copy(
        out=grouped.rearrange("p (c i) t -> p c t i", i=WEIGHT_RUN),
        in_=rows.rearrange("p t (c i) -> p c t i", i=WEIGHT_RUN),
    )


def tile_graphmessagelayer_pa_k_kernel(tc, node_state, positions, We1, be1, We2, be2, out):
    nc = tc.nc
    with ExitStack() as ctx:
        keep = ctx.enter_context(tc.tile_pool(name="keep", bufs=1))
        loads = ctx.enter_context(tc.tile_pool(name="loads", bufs=6))
        groupeds = ctx.enter_context(tc.tile_pool(name="groupeds", bufs=4))
        work = ctx.enter_context(tc.tile_pool(name="work", bufs=2))
        terms = ctx.enter_context(tc.tile_pool(name="terms", bufs=6))
        pres = ctx.enter_context(tc.tile_pool(name="pres", bufs=4))
        banks = ctx.enter_context(tc.psum_pool(name="banks", bufs=4))
        sums = ctx.enter_context(tc.psum_pool(name="sums", bufs=1))

        x_rows = keep.tile([P, FEATURES], BF16)
        nc.sync.dma_start(out=x_rows[:], in_=node_state.rearrange("b n h -> (b n) h"))
        pos_own = keep.tile([P, COORDS], BF16)
        nc.scalar.dma_start(out=pos_own[:], in_=positions.rearrange("b n c -> (b n) c"))
        pos_graph = keep.tile([P, NODES_PER_GRAPH * COORDS], BF16)
        for b in range(GRAPHS):
            nc.scalar.dma_start(
                out=pos_graph[b * NODES_PER_GRAPH : (b + 1) * NODES_PER_GRAPH, :],
                in_=positions[b].rearrange("n c -> (n c)").partition_broadcast(NODES_PER_GRAPH),
            )
        vec_rows = keep.tile([P, P], BF16)
        nc.scalar.dma_start(
            out=vec_rows[0:HIDDEN_TILES, :],
            in_=We1[2 * FEATURES : 2 * FEATURES + 1, :].rearrange("o (q p) -> (o q) p", p=P),
        )
        nc.scalar.dma_start(out=vec_rows[HIDDEN_TILES:P, :], in_=be1.rearrange("(q p) -> q p", p=P))
        be2_all = keep.tile([P, MESSAGE], BF16)
        nc.scalar.dma_start(out=be2_all[:], in_=be2.partition_broadcast(P))

        ident_bf16 = keep.tile([P, P], BF16)
        make_identity(nc, ident_bf16[:])
        ident_f32 = keep.tile([P, P], F32)
        make_identity(nc, ident_f32[:])

        xT = banks.tile([P, PACK, NODES], BF16, tag="bank")
        for t in range(PACK):
            nc.tensor.transpose(out=xT[:, t, :], in_=x_rows[:, t * P : (t + 1) * P], identity=ident_bf16[:])
        x_words = keep.tile([P, NODES, PACK], BF16)
        nc.vector.tensor_copy(out=x_words[:], in_=xT[:].rearrange("p t n -> p n t"))

        xi_in = work.tile([P, J_PER_CHUNK, NODES, PACK], BF16, tag="h_bf16", bufs=3, align_bytes=64)
        nc.vector.tensor_copy(
            out=xi_in[:], in_=x_words[:].unsqueeze(1).to_broadcast([P, J_PER_CHUNK, NODES, PACK])
        )
        xi_codes = keep.tile([P, EDGE_CHUNK], U32, align_bytes=256)
        xi_scales = keep.tile([P, EDGE_CHUNK], U8, align_bytes=256)
        nc.vector.quantize_mx(
            out=xi_codes[:].bitcast(FP8X4),
            scales=xi_scales[:],
            in_=xi_in[:].rearrange("p s n t -> p (s n t)"),
        )

        xj_codes = keep.tile([P, EDGE_CHUNKS, EDGE_CHUNK], U32, align_bytes=256)
        xj_scales = keep.tile([P, EDGE_CHUNKS, EDGE_CHUNK], U8, align_bytes=256)
        x_by_graph = x_words[:].rearrange("p (b n) t -> p b n t", n=NODES_PER_GRAPH)
        for c in range(EDGE_CHUNKS):
            xj_in = work.tile([P, J_PER_CHUNK, GRAPHS, NODES_PER_GRAPH, PACK], BF16, tag="h_bf16", bufs=3, align_bytes=64)
            for s in range(J_PER_CHUNK):
                j = c * J_PER_CHUNK + s
                nc.vector.tensor_copy(
                    out=xj_in[:, s],
                    in_=x_by_graph[:, :, j : j + 1, :].to_broadcast([P, GRAPHS, NODES_PER_GRAPH, PACK]),
                )
            nc.vector.quantize_mx(
                out=xj_codes[:, c, :].bitcast(FP8X4),
                scales=xj_scales[:, c, :],
                in_=xj_in[:].rearrange("p s b i t -> p (s b i t)"),
            )

        vecT = banks.tile([P, P], BF16, tag="bank")
        nc.tensor.transpose(out=vecT[:], in_=vec_rows[:], identity=ident_bf16[:])
        vec_cols = keep.tile([P, P], F32)
        nc.vector.tensor_copy(out=vec_cols[:], in_=vecT[:])
        w_dist = vec_cols[:, 0:HIDDEN_TILES].rearrange("p (g t) -> p g t", t=PACK)
        be1_cols = vec_cols[:, HIDDEN_TILES:P].rearrange("p (g t) -> p g t", t=PACK)
        be1_rest = keep.tile([P, HIDDEN_PASSES, PACK], F32)
        nc.vector.tensor_tensor(
            out=be1_rest[:],
            in0=be1_cols,
            in1=be1_cols[:, :, LAST : LAST + 1].to_broadcast([P, HIDDEN_PASSES, PACK]),
            op=ALU.subtract,
        )

        rel = keep.tile([P, NODES_PER_GRAPH, COORDS], F32)
        nc.vector.tensor_tensor(
            out=rel[:],
            in0=pos_graph[:].rearrange("p (n c) -> p n c", c=COORDS),
            in1=pos_own[:].unsqueeze(1).to_broadcast([P, NODES_PER_GRAPH, COORDS]),
            op=ALU.subtract,
        )
        rel_sq = keep.tile([P, NODES_PER_GRAPH, COORDS], F32)
        nc.vector.tensor_tensor(out=rel_sq[:], in0=rel[:], in1=rel[:], op=ALU.mult)
        sq = keep.tile([P, NODES_PER_GRAPH], F32)
        nc.vector.tensor_reduce(out=sq[:], in_=rel_sq[:], axis=mybir.AxisListType.X, op=ALU.add)
        sq_safe = keep.tile([P, NODES_PER_GRAPH], F32)
        nc.vector.tensor_scalar_max(out=sq_safe[:], in0=sq[:], scalar1=SMALLEST_SQUARE)
        root = keep.tile([P, NODES_PER_GRAPH], F32)
        nc.scalar.activation(out=root[:], in_=sq_safe[:], func=ACT.Sqrt)
        dist = keep.tile([P, NODES_PER_GRAPH], F32)
        nc.vector.scalar_tensor_tensor(
            out=dist[:], in0=sq[:], scalar=0.0, in1=root[:], op0=ALU.is_gt, op1=ALU.mult
        )
        dist_rep = pres.tile([P, NODES_PER_GRAPH, P], F32, tag="pre")
        nc.vector.tensor_copy(out=dist_rep[:], in_=dist[:].unsqueeze(2).to_broadcast([P, NODES_PER_GRAPH, P]))
        dist_all = keep.tile([P, EDGE_CHUNKS, EDGE_CHUNK], F32)
        for c in range(EDGE_CHUNKS):
            distT = banks.tile([P, J_PER_CHUNK, NODES], F32, tag="bank")
            for s in range(J_PER_CHUNK):
                nc.tensor.transpose(
                    out=distT[:, s, :], in_=dist_rep[:, c * J_PER_CHUNK + s, :], identity=ident_f32[:]
                )
            nc.scalar.copy(out=dist_all[:, c, :], in_=distT[:].rearrange("p s n -> p (s n)"))

        we1_codes = [keep.tile([P, HIDDEN], U32, name="we1_codes%d" % blk, align_bytes=256) for blk in range(2)]
        we1_scales = [keep.tile([P, HIDDEN], U8, name="we1_scales%d" % blk, align_bytes=256) for blk in range(2)]
        we2_codes = keep.tile([P, HIDDEN_PASSES, MESSAGE], U32, align_bytes=256)
        we2_scales = keep.tile([P, HIDDEN_PASSES, MESSAGE], U8, align_bytes=256)
        we2_view = We2.rearrange("(g t p) m -> p g t m", t=PACK, p=P)

        def quantise_we1(g):
            cols = slice(g * K_PASS, (g + 1) * K_PASS)
            for blk, copy in ((0, nc.vector.tensor_copy), (1, nc.scalar.copy)):
                rows = loads.tile([P, PACK, K_PASS], BF16, tag="rows")
                block = We1[blk * FEATURES : (blk + 1) * FEATURES, :].rearrange("(t p) f -> p t f", p=P)
                nc.sync.dma_start(out=rows[:], in_=block[:, :, cols])
                grouped = groupeds.tile([P, K_PASS, PACK], BF16, tag="grouped", align_bytes=64)
                regroup(copy, grouped[:], rows[:])
                nc.vector.quantize_mx(
                    out=we1_codes[blk][:, cols].bitcast(FP8X4),
                    scales=we1_scales[blk][:, cols],
                    in_=grouped[:].rearrange("p f t -> p (f t)"),
                )

        def quantise_we2(first_pass):
            passes = slice(first_pass, first_pass + WE2_PASSES)
            rows = loads.tile([P, WE2_PASSES, PACK, MESSAGE], BF16, tag="rows")
            nc.sync.dma_start(out=rows[:], in_=we2_view[:, passes])
            grouped = groupeds.tile([P, WE2_PASSES, MESSAGE, PACK], BF16, tag="grouped", align_bytes=64)
            for g in range(WE2_PASSES):
                regroup(nc.scalar.copy, grouped[:, g], rows[:, g])
            nc.vector.quantize_mx(
                out=we2_codes[:, passes, :].rearrange("p g m -> p (g m)").bitcast(FP8X4),
                scales=we2_scales[:, passes, :].rearrange("p g m -> p (g m)"),
                in_=grouped[:].rearrange("p g m t -> p (g m t)"),
            )

        def prepare_weights(g):
            quantise_we1(g)
            if g % WE2_PASSES == 0:
                quantise_we2(g)

        out_rows = out.rearrange("b i j m -> (b i) j m")
        prepare_weights(0)
        for c in range(EDGE_CHUNKS):
            msg = [sums.tile([P, MESSAGE], F32, name="msg%d" % s) for s in range(J_PER_CHUNK)]
            for g in range(HIDDEN_PASSES):
                if c == 0 and g + 1 < HIDDEN_PASSES:
                    prepare_weights(g + 1)

                pre = pres.tile([P, PACK, EDGE_CHUNK], F32)
                for t in range(PACK):
                    q = g * PACK + t
                    f_cols = slice(q * P, (q + 1) * P)
                    node_terms = banks.tile([P, EDGE_CHUNK], F32, tag="bank")
                    nc.tensor.matmul_mx(
                        out=node_terms[:],
                        lhsT=we1_codes[0][:, f_cols].bitcast(FP8X4),
                        lhsT_scale=we1_scales[0][:, f_cols],
                        rhs=xi_codes[:].bitcast(FP8X4),
                        rhs_scale=xi_scales[:],
                        start=True,
                        stop=False,
                    )
                    nc.tensor.matmul_mx(
                        out=node_terms[:],
                        lhsT=we1_codes[1][:, f_cols].bitcast(FP8X4),
                        lhsT_scale=we1_scales[1][:, f_cols],
                        rhs=xj_codes[:, c, :].bitcast(FP8X4),
                        rhs_scale=xj_scales[:, c, :],
                        start=False,
                        stop=True,
                    )
                    if t == LAST:
                        nc.vector.scalar_tensor_tensor(
                            out=pre[:, t, :], in0=dist_all[:, c, :], scalar=w_dist[:, g, t : t + 1],
                            in1=node_terms[:], op0=ALU.mult, op1=ALU.add,
                        )
                    else:
                        dist_term = terms.tile([P, EDGE_CHUNK], F32)
                        if t == SHARED and g % 2 == 1:
                            nc.scalar.activation(
                                out=dist_term[:], in_=dist_all[:, c, :], func=ACT.Identity,
                                scale=w_dist[:, g, t : t + 1], bias=be1_rest[:, g, t : t + 1],
                            )
                        else:
                            nc.gpsimd.tensor_scalar(
                                out=dist_term[:], in0=dist_all[:, c, :], scalar1=w_dist[:, g, t : t + 1],
                                scalar2=be1_rest[:, g, t : t + 1], op0=ALU.mult, op1=ALU.add,
                            )
                        nc.vector.tensor_tensor(out=pre[:, t, :], in0=node_terms[:], in1=dist_term[:], op=ALU.add)

                h_bf16 = work.tile([P, EDGE_CHUNK, PACK], BF16, bufs=3, align_bytes=64)
                nc.scalar.activation(
                    out=h_bf16[:].rearrange("p (c i) t -> p c t i", i=RUN),
                    in_=pre[:].rearrange("p t (c i) -> p c t i", i=RUN),
                    func=ACT.Silu,
                    bias=be1_cols[:, g, LAST : LAST + 1],
                )
                h_codes = work.tile([P, EDGE_CHUNK], U32, bufs=3, align_bytes=256)
                h_scales = work.tile([P, EDGE_CHUNK], U8, bufs=3, align_bytes=256)
                nc.vector.quantize_mx(
                    out=h_codes[:].bitcast(FP8X4),
                    scales=h_scales[:],
                    in_=h_bf16[:].rearrange("p e t -> p (e t)"),
                )
                for s in range(J_PER_CHUNK):
                    e_cols = slice(s * NODES, (s + 1) * NODES)
                    nc.tensor.matmul_mx(
                        out=msg[s][:],
                        lhsT=h_codes[:, e_cols].bitcast(FP8X4),
                        lhsT_scale=h_scales[:, e_cols],
                        rhs=we2_codes[:, g, :].bitcast(FP8X4),
                        rhs_scale=we2_scales[:, g, :],
                        start=(g == 0),
                        stop=(g == HIDDEN_PASSES - 1),
                    )

            result = work.tile([P, J_PER_CHUNK, MESSAGE], F32)
            for s in range(J_PER_CHUNK):
                nc.vector.tensor_tensor(out=result[:, s, :], in0=msg[s][:], in1=be2_all[:], op=ALU.add)
            nc.sync.dma_start(out=out_rows[:, c * J_PER_CHUNK : (c + 1) * J_PER_CHUNK, :], in_=result[:])
